import numpy as np
import ml_dtypes


def mxq(x, axis, fmt="e4m3"):
    dtype, down = {"e4m3": (ml_dtypes.float8_e4m3fn, 7), "e5m2": (ml_dtypes.float8_e5m2, 14)}[fmt]
    v = np.moveaxis(np.asarray(x, np.float32).astype(ml_dtypes.bfloat16).astype(np.float64), axis, -1)
    blocks = v.reshape(v.shape[:-1] + (-1, 32))
    amax = np.abs(blocks).max(-1, keepdims=True)
    byte = np.maximum(np.where(amax > 0, np.frexp(amax)[1] - 1 + 127, 0) - down, 1)
    scale = np.exp2(byte - 127.0)
    codes = (blocks / scale).astype(np.float32).astype(dtype).astype(np.float64)
    return np.moveaxis((codes * scale).reshape(v.shape), -1, axis)


WIDE = False


def mx_kscale(k):
    if not WIDE:
        return np.ones(k)
    levels = np.array([10, -10, 5, -5, 0])
    if k % 512:
        return np.exp2(np.random.permutation(np.resize(levels, k // 32))).repeat(32)
    a = np.empty((k // 512, 16))
    for p in range(k // 512):
        a[p, :8] = np.random.permutation(np.resize(levels, 8))
        for g in range(8):
            far = levels[np.abs(levels - a[p, g]) >= 10]
            a[p, g + 8] = far[np.random.randint(len(far))]
    return np.exp2(a.ravel()).repeat(32)


BF16 = ml_dtypes.bfloat16


def bf(x):
    return np.asarray(x, np.float32).astype(BF16)


def f64(x):
    return np.asarray(x).astype(np.float64)


B, N, D, H, HD, S, DO = 1, 1536, 1024, 16, 64, 11, 1024
E = H * HD
D4 = [0.4829629131445341, 0.8365163037378079, 0.2241438680420134, -0.1294095225512604]
T = len(D4)


def elu1(u):
    return np.where(u > 0.0, u, np.exp(np.minimum(u, 0.0)) - 1.0) + 1.0


def softplus(u):
    return np.log(1.0 + np.exp(u))


def shifted(t, o):
    if o == 0:
        return t
    return np.concatenate([np.zeros((B, H, o, HD)), t[:, :, :N - o, :]], axis=2)


def setup_inputs():
    s = mx_kscale(D)
    lg = np.random.standard_normal((B, H, N, S)) * 1.4
    g = np.exp(lg - lg.max(-1, keepdims=True))
    return {"x": bf(np.random.standard_normal((B, N, D)) * s),
            "W_qkv": bf(np.random.standard_normal((3 * E, D)) * 0.6 / np.sqrt(D) / s),
            "b_qkv": bf(np.random.standard_normal(3 * E) * 0.1),
            "gains": bf(g / g.sum(-1, keepdims=True)),
            "pos_bias": bf(np.random.standard_normal((S * T, H)) * 0.5),
            "identity_bypass": bf(-1.0 + 0.5 * np.random.standard_normal(H))}


def core(x, W_qkv, b_qkv, gains, pos_bias, identity_bypass):
    qkv = (mxq(f64(x), 2, "e4m3") @ mxq(f64(W_qkv), 1, "e4m3").T) + f64(b_qkv)
    q, k, v = [t.reshape(B, N, H, HD).transpose(0, 2, 1, 3) for t in np.split(qkv, 3, axis=-1)]
    g, pb = f64(gains), f64(pos_bias)
    acc = np.zeros((B, H, N, HD))
    z = np.zeros((B, H, N, 1))
    tap = 0
    for j in range(S):
        d = 1 << j
        g_j = g[..., j][..., None]
        for tau, c in enumerate(D4):
            o = d * tau
            bias = pb[tap].reshape(1, H, 1, 1)
            tap += 1
            if o != 0 and o >= N:
                continue
            k_s, v_s = shifted(k, o), shifted(v, o)
            feat = elu1(np.sum(q * k_s, -1, keepdims=True) + bias)
            acc = acc + (g_j * c) * feat * v_s
            z = z + g_j * abs(c) * feat
    p = softplus(f64(identity_bypass)).reshape(1, H, 1, 1)
    local = elu1(np.sum(q * k, -1, keepdims=True))
    acc = acc + p * local * v
    z = z + p * local
    res = acc / (z + 1e-06)
    return res.transpose(0, 2, 1, 3).reshape(B, N, E)


def e4m3fn_bytes(y):
    return np.clip(np.asarray(y, np.float64), -448.0, 448.0).astype(np.float32).astype(ml_dtypes.float8_e4m3fn).view(np.uint8)


def reference(x, W_qkv, b_qkv, gains, pos_bias, identity_bypass):
    out = core(x, W_qkv, b_qkv, gains, pos_bias, identity_bypass)
    s = np.max(np.abs(out), axis=-1, keepdims=True) / 448.0
    return out, e4m3fn_bytes(out / s)

@@ -1,0 +1,564 @@
+from contextlib import ExitStack
+
+import concourse.mybir as mybir
+from concourse.masks import make_identity
+
+F32 = mybir.dt.float32
+BF16 = mybir.dt.bfloat16
+U32 = mybir.dt.uint32
+U8 = mybir.dt.uint8
+FP8X4 = mybir.dt.float8_e4m3fn_x4
+FP8 = mybir.dt.float8_e4m3fn
+ALU = mybir.AluOpType
+ACT = mybir.ActivationFunctionType
+AX = mybir.AxisListType
+
+P = 128
+NTOK = 1536
+NT = 12
+DM = 1024
+E = 1024
+H = 16
+HD = 64
+PAD = 128
+D4 = [0.4829629131445341, 0.8365163037378079, 0.2241438680420134, -0.1294095225512604]
+OFFS = [0, 1, 2, 4, 8, 16, 32, 64, 128, 256, 512, 1024, 3, 6, 12, 24, 48, 96, 192, 384, 768]
+NOFF = 21
+NSLOT = 43
+BIG = 3.0e38
+
+FLOPS = 2 * NTOK * 3 * E * DM + 4 * NTOK * E * NOFF
+
+TILE_ORDER = [0, 2, 3, 4, 5, 6, 7, 8, 9, 10, 11, 1]
+SPLIT = {0: (12, 4), 2: (12, 4), 3: (12, 4), 4: (12, 4), 5: (12, 4), 6: (12, 4), 7: (12, 4), 8: (12, 4),
+         9: (12, 4), 10: (12, 4), 11: (8, 4), 1: (8, 4)}
+
+C_PRE = 0
+C_RED = 1
+C_SW = 2
+C_QP = 3
+C_M1 = 4
+C_SH = 5
+C_QKT = 6
+C_MUL = 7
+C_ADD = 8
+C_F1 = 9
+C_FIN = 10
+
+
+def valid_ids(t):
+    return [i for i in range(NOFF) if OFFS[i] < P * (t + 1)]
+
+
+def build_plan():
+    plan = {}
+
+    def at(step, cls, item):
+        plan.setdefault((step, cls), []).append(item)
+
+    ready = {}
+    n = 0
+    for t in TILE_ORDER:
+        ids = valid_ids(t)
+        at(n, C_PRE, ("pre", t))
+        at(n, C_QP, ("qp", t))
+        for grp in ([i for i in ids if i < 12], [i for i in ids if i >= 12]):
+            for c0 in range(0, len(grp), 4):
+                ch = grp[c0:c0 + 4]
+                for sl, i in enumerate(ch):
+                    at(n, C_M1, ("m1", t, i))
+                    at(n + 1, C_QKT, ("qkt", t, i, sl))
+                    if sl == len(ch) - 1:
+                        at(n + 2, C_RED, ("red", t, ch[0], len(ch)))
+                    n += 1
+        last = n - 1
+        at(last + 2, C_SW, ("sw1", t))
+        at(last + 4, C_SW, ("sw2", t))
+        at(last + 6, C_SW, ("sw3", t))
+        at(last + 8, C_SW, ("sw4", t))
+        at(last + 9, C_SW, ("sw5", t))
+        at(last + 10, C_SW, ("sw6", t))
+        ready[t] = last + 12
+
+    def place_fin(t, f):
+        at(f, C_SH, ("bt", t))
+        at(f + 1, C_MUL, ("f2", t))
+        at(f + 2, C_FIN, ("f3", t))
+        at(f + 3, C_FIN, ("f4", t))
+
+    cur = 0
+    pend = []
+    for t in TILE_ORDER:
+        ids = valid_ids(t)
+        for k, i in enumerate(ids):
+            step = max(cur, ready[t])
+            if pend and pend[0][1] <= step:
+                f = max(cur, pend[0][1])
+                place_fin(pend[0][0], f)
+                pend = []
+                cur = f + 1
+                step = max(cur, ready[t])
+            first = k == 0
+            last = k == len(ids) - 1
+            if OFFS[i] % P != 0:
+                at(step - 2, C_SH, ("sh", t, i))
+            at(step + 1, C_MUL, ("mul", t, i))
+            at(step + 2, C_ADD, ("add", t, i, first, last))
+            if last:
+                at(step + 2, C_F1, ("f1", t))
+                pend = [(t, step + 3)]
+            cur = step + 1
+    place_fin(pend[0][0], max(cur, pend[0][1]))
+    return plan
+
+
+def tile_dwarfattention_pa_kernel(tc, x, W_qkv, b_qkv, gains, pos_bias, identity_bypass, out_0, out_1):
+    nc = tc.nc
+    x2 = x.flatten_outer_dims()
+    o0_dram = out_0.flatten_outer_dims()
+    o1_dram = out_1.flatten_outer_dims()
+
+    with ExitStack() as ctx:
+        keep = ctx.enter_context(tc.tile_pool(name="keep", bufs=1))
+
+        ident = keep.tile([P, P], F32, name="ident")
+        make_identity(nc, ident[:])
+
+        qA = keep.tile([P, NT, E], F32, name="qA")
+        kT = keep.tile([P, 8, PAD + NTOK], F32, name="kT")
+        vA = keep.tile([P, NT, E], F32, name="vA")
+        graw = keep.tile([P, 11, H, NT], BF16, name="graw")
+        bk = keep.tile([P, 8], F32, name="bk")
+        biasB = keep.tile([P, NSLOT, H], F32, name="biasB")
+        gw_tiles = [keep.tile([P, NSLOT, H], F32, name="gw0"), keep.tile([P, NSLOT, H], F32, name="gw1")]
+        nc.gpsimd.memset(kT[:, :, 0:PAD], 0.0)
+
+        with ExitStack() as p0:
+            rawp = p0.enter_context(tc.tile_pool(name="rawp", bufs=4))
+            xgp = p0.enter_context(tc.tile_pool(name="xgp", bufs=2))
+            wgp = p0.enter_context(tc.tile_pool(name="wgp", bufs=2))
+            wcp = p0.enter_context(tc.tile_pool(name="wcp", bufs=4))
+            mvp = p0.enter_context(tc.tile_pool(name="mvp", bufs=2))
+            cod = p0.enter_context(tc.tile_pool(name="cod", bufs=1))
+            pst = p0.enter_context(tc.psum_pool(name="pst", bufs=3))
+            psm = p0.enter_context(tc.psum_pool(name="psm", bufs=4))
+
+            bkraw = cod.tile([P, 8], BF16, name="bkraw")
+            pbraw = cod.tile([P, 44 * H], BF16, name="pbraw")
+            ibraw = cod.tile([P, H], BF16, name="ibraw")
+            nc.scalar.dma_start(out=bkraw[:], in_=b_qkv[E:2 * E].rearrange("(j a) -> j a", a=8))
+            nc.scalar.dma_start(out=pbraw[:], in_=pos_bias.rearrange("r h -> (r h)").partition_broadcast(P))
+            nc.scalar.dma_start(out=ibraw[:], in_=identity_bypass.partition_broadcast(P))
+            identb = cod.tile([P, P], BF16, name="identb")
+            make_identity(nc, identb[:])
+            gr = [cod.tile([P, P * 11], BF16, name="gr0"), cod.tile([P, P * 11], BF16, name="gr1")]
+            for half in range(2):
+                nc.gpsimd.memset(gr[half][96:P, :], 0.0)
+                nc.scalar.dma_start(
+                    out=gr[half][0:96, :],
+                    in_=gains[0, 8 * half:8 * half + 8, :, :].rearrange("h (t n) j -> (h t) (n j)", t=NT),
+                )
+            graw_q = graw[:].rearrange("p j h t -> p (j h t)").rearrange("p (q c) -> p q c", c=96)
+            for q0 in range(0, 22, 4):
+                nq = min(4, 22 - q0)
+                gp = pst.tile([P, 4, P], BF16, name="tp")
+                for k in range(nq):
+                    nc.tensor.transpose(gp[:, k, :], gr[(q0 + k) % 2][:, (q0 + k) // 2:P * 11:11], identb[:])
+                nc.vector.tensor_copy(out=graw_q[:, q0:q0 + nq, :], in_=gp[:, 0:nq, 0:96])
+
+            nc.vector.tensor_copy(out=bk[:], in_=bkraw[:])
+
+            pb4 = pbraw[:].rearrange("p (j c h) -> p j c h", c=4, h=H)
+            nc.vector.memset(biasB[:, 11:13, :], 0.0)
+            nc.vector.tensor_copy(out=biasB[:, 0:11, :], in_=pb4[:, :, 0, :])
+            nc.vector.tensor_copy(out=biasB[:, 13:23, :], in_=pb4[:, 0:10, 2, :])
+            nc.vector.tensor_copy(out=biasB[:, 23:34, :], in_=pb4[:, :, 1, :])
+            nc.vector.tensor_copy(out=biasB[:, 34:43, :], in_=pb4[:, 0:9, 3, :])
+
+            ib = cod.tile([P, H], F32, name="ib")
+            sp_a = cod.tile([P, H], F32, name="sp_a")
+            nc.vector.tensor_copy(out=ib[:], in_=ibraw[:])
+            nc.scalar.activation(out=sp_a[:], in_=ib[:], func=ACT.Abs)
+            nc.scalar.activation(out=sp_a[:], in_=sp_a[:], func=ACT.Exp, scale=-1.0)
+            nc.vector.tensor_scalar(out=sp_a[:], in0=sp_a[:], scalar1=1.0, scalar2=None, op0=ALU.add)
+            nc.scalar.activation(out=sp_a[:], in_=sp_a[:], func=ACT.Ln)
+            for gw in gw_tiles:
+                nc.vector.memset(gw[:, 12, :], 0.0)
+                nc.vector.scalar_tensor_tensor(
+                    out=gw[:, 11, :], in0=ib[:], scalar=0.0, in1=sp_a[:], op0=ALU.max, op1=ALU.add
+                )
+
+            xc = cod.tile([P, 2, NTOK], U32, name="xc", align_bytes=64)
+            xs = cod.tile([P, 2, NTOK], U8, name="xs", align_bytes=64)
+
+            bqB = cod.tile([P, E], F32, name="bqB")
+            bvB = cod.tile([P, E], F32, name="bvB")
+            bq_raw = rawp.tile([P, DM], BF16, name="raw")
+            nc.scalar.dma_start(out=bq_raw[:], in_=b_qkv[0:E].partition_broadcast(P))
+            nc.gpsimd.tensor_copy(
+                out=bqB[:].rearrange("p (a j) -> p a j", a=8), in_=bq_raw[:].rearrange("p (j a) -> p a j", a=8)
+            )
+            bv_raw = rawp.tile([P, DM], BF16, name="raw")
+            nc.scalar.dma_start(out=bv_raw[:], in_=b_qkv[2 * E:3 * E].partition_broadcast(P))
+            nc.gpsimd.tensor_copy(out=bvB[:], in_=bv_raw[:])
+
+            def turn(rows, dst_words):
+                raw = rawp.tile([P, DM], BF16, name="raw")
+                nc.sync.dma_start(out=raw[:], in_=rows)
+                words = raw[:].bitcast(F32)
+                tp = pst.tile([P, 2, 2, P], F32, name="tp")
+                for g in range(2):
+                    for u in range(2):
+                        nc.tensor.transpose(tp[:, g, u, :], words[:, 256 * g + u:256 * (g + 1):2], ident[:])
+                nc.scalar.copy(out=dst_words, in_=tp[:].rearrange("p g u r -> p g r u"))
+
+            def quantize_512(row_blocks, cd, sc):
+                xg = xgp.tile([P, 2, 512, 4], BF16, name="xg", align_bytes=64)
+                for r in range(4):
+                    turn(row_blocks[r], xg[:, :, r * P:(r + 1) * P, :].bitcast(F32))
+                for g in range(2):
+                    nc.vector.quantize_mx(
+                        out=cd[g].bitcast(FP8X4), scales=sc[g], in_=xg[:, g, :, :].rearrange("p r j -> p (r j)")
+                    )
+
+            for c in range(3):
+                cols = slice(c * 512, (c + 1) * 512)
+                quantize_512(
+                    [x2[c * 512 + r * P:c * 512 + (r + 1) * P, :] for r in range(4)],
+                    [xc[:, g, cols] for g in range(2)],
+                    [xs[:, g, cols] for g in range(2)],
+                )
+
+            wq_view = W_qkv[0:E, :].rearrange("(j a) k -> a j k", a=8)
+            wk_view = W_qkv[E:2 * E, :].rearrange("(j a) k -> a j k", a=8)
+            codes = {}
+
+            def prep_k(a):
+                wg = wgp.tile([P, 2, P, 4], BF16, name="wg", align_bytes=64)
+                turn(wk_view[a], wg[:].bitcast(F32))
+                wc = wcp.tile([P, 2 * P], U32, name="wc", align_bytes=64)
+                ws = wcp.tile([P, 2 * P], U8, name="ws", align_bytes=64)
+                nc.vector.quantize_mx(
+                    out=wc[:].bitcast(FP8X4), scales=ws[:], in_=wg[:].rearrange("p g r j -> p (g r j)")
+                )
+                codes[a] = (wc, ws)
+
+            def project_k(a):
+                wc, ws = codes[a]
+                for c in range(3):
+                    cols = slice(c * 512, (c + 1) * 512)
+                    acc = psm.tile([P, 512], F32, name="acc")
+                    for g in range(2):
+                        nc.tensor.matmul_mx(
+                            out=acc[:],
+                            lhsT=wc[:, g * P:(g + 1) * P].bitcast(FP8X4),
+                            lhsT_scale=ws[:, g * P:(g + 1) * P],
+                            rhs=xc[:, g, cols].bitcast(FP8X4),
+                            rhs_scale=xs[:, g, cols],
+                            start=(g == 0),
+                            stop=(g == 1),
+                        )
+                    nc.scalar.activation(
+                        out=kT[:, a, PAD + c * 512:PAD + (c + 1) * 512], in_=acc[:], func=ACT.Identity,
+                        bias=bk[:, a:a + 1], scale=1.0,
+                    )
+
+            def prep_moving(key, row_blocks):
+                mc = mvp.tile([P, 2, 512], U32, name="mc", align_bytes=64)
+                ms = mvp.tile([P, 2, 512], U8, name="ms", align_bytes=64)
+                quantize_512(row_blocks, [mc[:, g, :] for g in range(2)], [ms[:, g, :] for g in range(2)])
+                codes[key] = (mc, ms)
+
+            def project_tokens(key, dst, bias_row, c):
+                mc, ms = codes[key]
+                cols = slice(c * 512, (c + 1) * 512)
+                for tt in range(NT):
+                    acc = psm.tile([P, 512], F32, name="acc")
+                    for g in range(2):
+                        nc.tensor.matmul_mx(
+                            out=acc[:],
+                            lhsT=xc[:, g, tt * P:(tt + 1) * P].bitcast(FP8X4),
+                            lhsT_scale=xs[:, g, tt * P:(tt + 1) * P],
+                            rhs=mc[:, g, :].bitcast(FP8X4),
+                            rhs_scale=ms[:, g, :],
+                            start=(g == 0),
+                            stop=(g == 1),
+                        )
+                    nc.vector.tensor_tensor(out=dst[:, tt, cols], in0=acc[:], in1=bias_row[:, cols], op=ALU.add)
+
+            def q_blocks(c):
+                return [wq_view[4 * c + r] for r in range(4)]
+
+            def v_blocks(c):
+                return [W_qkv[2 * E + c * 512 + r * P:2 * E + c * 512 + (r + 1) * P, :] for r in range(4)]
+
+            prep_k(0)
+            prep_k(1)
+            for a0 in range(0, 8, 2):
+                if a0 + 2 < 8:
+                    prep_k(a0 + 2)
+                    prep_k(a0 + 3)
+                else:
+                    prep_moving("q0", q_blocks(0))
+                project_k(a0)
+                project_k(a0 + 1)
+            prep_moving("q1", q_blocks(1))
+            project_tokens("q0", qA, bqB, 0)
+            prep_moving("v0", v_blocks(0))
+            project_tokens("q1", qA, bqB, 1)
+            prep_moving("v1", v_blocks(1))
+            project_tokens("v0", vA, bvB, 0)
+            project_tokens("v1", vA, bvB, 1)
+
+        with ExitStack() as p1:
+            ptp = p1.enter_context(tc.tile_pool(name="ptp", bufs=3))
+            tmpp = p1.enter_context(tc.tile_pool(name="tmpp", bufs=3))
+            vop = p1.enter_context(tc.tile_pool(name="vop", bufs=4))
+            sp3 = p1.enter_context(tc.tile_pool(name="sp3", bufs=3))
+            sp2 = p1.enter_context(tc.tile_pool(name="sp2", bufs=2))
+            sp1 = p1.enter_context(tc.tile_pool(name="sp1", bufs=1))
+            sps = p1.enter_context(tc.psum_pool(name="sps", bufs=2))
+            one = p1.enter_context(tc.psum_pool(name="one", bufs=1))
+
+            pos_of = {}
+            for k, t in enumerate(TILE_ORDER):
+                pos_of[t] = k
+            S = {}
+            QP = {}
+            PT = {}
+            SP = {}
+            UE = {}
+            ZW = {}
+            RZ = {}
+            W = {}
+            VO = {}
+            TMP = {}
+            ACC = {}
+            ACS = {}
+            BP = {}
+            O0 = {}
+            R = {}
+
+            def win(t, i):
+                lo = PAD + t * P - OFFS[i]
+                return slice(lo, lo + P)
+
+            def do_pre(t):
+                s = sp2.tile([P, NOFF, H], F32, name="s")
+                S[t] = s
+                ids = valid_ids(t)
+                na = len([i for i in ids if i < 12])
+                nb = len(ids) - na
+                if na < 12:
+                    nc.gpsimd.memset(s[:, na:12, :], 0.0)
+                if nb < 9:
+                    nc.gpsimd.memset(s[:, 12 + nb:NOFF, :], 0.0)
+                gw = gw_tiles[pos_of[t] % 2]
+                for (lo, nj, c) in ((0, 11, D4[0]), (13, 10, D4[2]), (23, 11, D4[1]), (34, 9, -D4[3])):
+                    nc.gpsimd.tensor_scalar(
+                        out=gw[:, lo:lo + nj, :],
+                        in0=graw[:, 0:nj, :, t],
+                        scalar1=c,
+                        scalar2=0.0,
+                        op0=ALU.mult,
+                        op1=ALU.add,
+                    )
+
+            def do_qp(t):
+                qp0 = one.tile([P, 4, P], F32, name="qp0")
+                qp1 = one.tile([P, 4, P], F32, name="qp1")
+                QP[t] = (qp0, qp1)
+                for a in range(8):
+                    nc.tensor.transpose(QP[t][a // 4][:, a % 4, :], qA[:, t, a * P:(a + 1) * P], ident[:])
+
+            def do_m1(t, i):
+                pt = ptp.tile([P, 8, P], F32, name="pt")
+                PT[(t, i)] = pt
+                for b in range(2):
+                    nc.vector.tensor_tensor(
+                        out=pt[:, 4 * b:4 * b + 4, :], in0=QP[t][b][:], in1=kT[:, 4 * b:4 * b + 4, win(t, i)],
+                        op=ALU.mult,
+                    )
+
+            def do_qkt(t, i, sl):
+                if sl == 0:
+                    SP[t] = sps.tile([P, 512], F32, name="sp")
+                sp = SP[t]
+                pt = PT[(t, i)]
+                for a in range(8):
+                    nc.tensor.matmul(
+                        out=sp[:, sl * P:(sl + 1) * P],
+                        lhsT=pt[:, a, :],
+                        rhs=ident[:],
+                        is_transpose=(a != 0),
+                        start=(a == 0),
+                        stop=(a == 7),
+                    )
+
+            def do_red(t, i0, n):
+                nc.vector.tensor_reduce(
+                    out=S[t][:, i0:i0 + n, :].rearrange("p a b -> p (a b)"),
+                    in_=SP[t][:, 0:n * P].rearrange("p (x l) -> p x l", l=8),
+                    axis=AX.X,
+                    op=ALU.add,
+                )
+
+            def do_sw1(t):
+                s = S[t]
+                u = sp1.tile([P, NSLOT, H], F32, name="u")
+                e = sp1.tile([P, NSLOT, H], F32, name="e")
+                r = sp1.tile([P, NSLOT, H], F32, name="r")
+                UE[t] = (u, e, r)
+                nc.gpsimd.tensor_tensor(
+                    out=u[:, 0:12, :], in0=s[:, 0:1, :].to_broadcast([P, 12, H]), in1=biasB[:, 0:12, :], op=ALU.add
+                )
+                nc.gpsimd.tensor_tensor(out=u[:, 12:23, :], in0=s[:, 1:12, :], in1=biasB[:, 12:23, :], op=ALU.add)
+                nc.gpsimd.tensor_tensor(out=u[:, 23:43, :], in0=s[:, 1:21, :], in1=biasB[:, 23:43, :], op=ALU.add)
+                nc.gpsimd.tensor_scalar(out=r[:], in0=u[:], scalar1=BIG, scalar2=0.0, op0=ALU.min, op1=ALU.max)
+
+            def do_sw2(t):
+                u, e, r = UE[t]
+                nc.scalar.activation(out=e[:], in_=u[:], func=ACT.Relu, scale=-1.0)
+                nc.scalar.activation(out=e[:], in_=e[:], func=ACT.Exp, scale=-1.0)
+
+            def do_sw3(t):
+                u, e, r = UE[t]
+                gw = gw_tiles[pos_of[t] % 2]
+                nc.gpsimd.tensor_tensor(out=r[:], in0=r[:], in1=e[:], op=ALU.add)
+                nc.gpsimd.tensor_tensor(out=e[:], in0=r[:], in1=gw[:], op=ALU.mult)
+
+            def do_sw4(t):
+                u, e, r = UE[t]
+                z = sp2.tile([P, H], F32, name="z")
+                wr = sp2.tile([P, 12, H], F32, name="wr")
+                ZW[t] = (z, wr)
+                nc.vector.tensor_reduce(out=z[:], in_=e[:].rearrange("p s h -> p h s"), axis=AX.X, op=ALU.add)
+                nc.vector.tensor_reduce(
+                    out=wr[:, 0, :], in_=e[:, 0:12, :].rearrange("p s h -> p h s"), axis=AX.X, op=ALU.add
+                )
+                nc.gpsimd.tensor_tensor(out=wr[:, 1:12, :], in0=e[:, 12:23, :], in1=e[:, 23:34, :], op=ALU.add)
+
+            def do_sw5(t):
+                z, wr = ZW[t]
+                rz = sp2.tile([P, H], F32, name="rz")
+                nrz = sp2.tile([P, H], F32, name="nrz")
+                RZ[t] = (rz, nrz)
+                nc.vector.tensor_scalar(out=z[:], in0=z[:], scalar1=1e-6, scalar2=None, op0=ALU.add)
+                nc.vector.reciprocal(out=rz[:], in_=z[:])
+                nc.vector.tensor_scalar(out=nrz[:], in0=rz[:], scalar1=-1.0, scalar2=None, op0=ALU.mult)
+
+            def do_sw6(t):
+                u, e, r = UE[t]
+                z, wr = ZW[t]
+                rz, nrz = RZ[t]
+                w = sp3.tile([P, NOFF, H], F32, name="w")
+                W[t] = w
+                nc.gpsimd.tensor_tensor(
+                    out=w[:, 0:12, :], in0=wr[:], in1=rz[:].unsqueeze(1).to_broadcast([P, 12, H]), op=ALU.mult
+                )
+                nc.gpsimd.tensor_tensor(
+                    out=w[:, 12:21, :], in0=e[:, 34:43, :], in1=nrz[:].unsqueeze(1).to_broadcast([P, 9, H]),
+                    op=ALU.mult,
+                )
+
+            def do_sh(t, i):
+                vo = vop.tile([P, E], F32, name="vo")
+                VO[(t, i)] = vo
+                a = OFFS[i] // P
+                r = OFFS[i] % P
+                pieces = [(r, 0, P - r, t - a)]
+                if t - a - 1 >= 0:
+                    pieces.append((0, P - r, r, t - a - 1))
+                else:
+                    nc.gpsimd.memset(vo[0:r, :], 0.0)
+                for (d0, s0, cnt, tile_ix) in pieces:
+                    big = cnt - cnt % 16
+                    for (off, n) in ((0, big), (big, cnt - big)):
+                        if n > 0:
+                            nc.sync.dma_start(
+                                out=vo[d0 + off:d0 + off + n, :], in_=vA[s0 + off:s0 + off + n, tile_ix, :]
+                            )
+
+            def do_mul(t, i):
+                hs, hg = SPLIT[t]
+                if OFFS[i] % P != 0:
+                    vo = VO[(t, i)][:]
+                else:
+                    vo = vA[:, t - OFFS[i] // P, :]
+                w = W[t]
+                tmp = tmpp.tile([P, E], F32, name="tmp")
+                TMP[(t, i)] = tmp
+                for (eng, h0, h1) in ((nc.gpsimd, hs, hs + hg), (nc.vector, hs + hg, H)):
+                    if h1 > h0:
+                        eng.tensor_tensor(
+                            out=tmp[:, h0 * HD:h1 * HD].rearrange("p (h d) -> p h d", d=HD),
+                            in0=vo[:, h0 * HD:h1 * HD].rearrange("p (h d) -> p h d", d=HD),
+                            in1=w[:, i, h0:h1].unsqueeze(2).to_broadcast([P, h1 - h0, HD]),
+                            op=ALU.mult,
+                        )
+                for h in range(hs):
+                    cols = slice(h * HD, (h + 1) * HD)
+                    nc.scalar.activation(out=tmp[:, cols], in_=vo[:, cols], func=ACT.Copy, scale=w[:, i, h:h + 1])
+
+            def do_add(t, i, first, last):
+                if first:
+                    acc0 = one.tile([P, 512], F32, name="acc0")
+                    acc1 = one.tile([P, 512], F32, name="acc1")
+                    ACC[t] = (acc0, acc1)
+                tmp = TMP[(t, i)]
+                for ft in range(8):
+                    nc.tensor.matmul(
+                        out=ACC[t][ft // 4][:, (ft % 4) * P:(ft % 4 + 1) * P],
+                        lhsT=tmp[:, ft * P:(ft + 1) * P],
+                        rhs=ident[:],
+                        is_transpose=True,
+                        start=(first and ft % 4 == 0),
+                        stop=(last and ft % 4 == 3),
+                    )
+
+            def do_f1(t):
+                acs = sp1.tile([P, E], F32, name="acs")
+                ACS[t] = acs
+                nc.vector.tensor_copy(out=acs[:, 0:512], in_=ACC[t][0][:])
+                nc.scalar.copy(out=acs[:, 512:E], in_=ACC[t][1][:])
+
+            def do_bt(t):
+                bp0 = one.tile([P, 512], F32, name="bp0")
+                bp1 = one.tile([P, 512], F32, name="bp1")
+                BP[t] = (bp0, bp1)
+                for ft in range(8):
+                    nc.tensor.transpose(
+                        BP[t][ft // 4][:, (ft % 4) * P:(ft % 4 + 1) * P], ACS[t][:, ft * P:(ft + 1) * P], ident[:]
+                    )
+
+            def do_f2(t):
+                O0[t] = sp2.tile([P, E], F32, name="o0")
+                nc.vector.tensor_copy(out=O0[t][:, 0:512], in_=BP[t][0][:])
+                nc.scalar.copy(out=O0[t][:, 512:E], in_=BP[t][1][:])
+
+            def do_f3(t):
+                am = sp2.tile([P, 1], F32, name="am")
+                r = sp2.tile([P, 1], F32, name="r448")
+                R[t] = r
+                nc.vector.tensor_reduce(out=am[:], in_=O0[t][:], axis=AX.X, op=ALU.max, apply_absolute_value=True)
+                nc.vector.reciprocal(out=r[:], in_=am[:])
+                nc.vector.tensor_scalar(out=r[:], in0=r[:], scalar1=448.0, scalar2=None, op0=ALU.mult)
+                nc.sync.dma_start(out=o0_dram[t * P:(t + 1) * P, :], in_=O0[t][:])
+
+            def do_f4(t):
+                o1 = sp2.tile([P, E], FP8, name="o1")
+                nc.vector.tensor_scalar(
+                    out=o1[:], in0=O0[t][:], scalar1=R[t][:, 0:1], scalar2=None, op0=ALU.mult, saturate=False
+                )
+                nc.sync.dma_start(out=o1_dram[t * P:(t + 1) * P, :], in_=o1[:].bitcast(U8))
+
+            table = {
+                "pre": do_pre, "qp": do_qp, "m1": do_m1, "qkt": do_qkt, "red": do_red, "sw1": do_sw1,
+                "sw2": do_sw2, "sw3": do_sw3, "sw4": do_sw4, "sw5": do_sw5, "sw6": do_sw6, "sh": do_sh,
+                "mul": do_mul, "add": do_add, "f1": do_f1, "bt": do_bt, "f2": do_f2, "f3": do_f3, "f4": do_f4,
+            }
+            plan = build_plan()
+            with tc.manual_schedule():
+                for key in sorted(plan.keys()):
+                    for item in plan[key]:
+                        table[item[0]](*item[1:])

@@ -101,7 +101,7 @@ def build_plan():
             first = k == 0
             last = k == len(ids) - 1
             if OFFS[i] % P != 0:
-                at(step - 2, C_SH, ("sh", t, i))
+                at(step - 4, C_SH, ("sh", t, i))
             at(step + 1, C_MUL, ("mul", t, i))
             at(step + 2, C_ADD, ("add", t, i, first, last))
             if last:
@@ -313,7 +313,7 @@ def tile_dwarfattention_pa_kernel(tc, x, W_qkv, b_qkv, gains, pos_bias, identity
         with ExitStack() as p1:
             ptp = p1.enter_context(tc.tile_pool(name="ptp", bufs=3))
             tmpp = p1.enter_context(tc.tile_pool(name="tmpp", bufs=3))
-            vop = p1.enter_context(tc.tile_pool(name="vop", bufs=4))
+            vop = p1.enter_context(tc.tile_pool(name="vop", bufs=6))
             sp3 = p1.enter_context(tc.tile_pool(name="sp3", bufs=3))
             sp2 = p1.enter_context(tc.tile_pool(name="sp2", bufs=2))
             sp1 = p1.enter_context(tc.tile_pool(name="sp1", bufs=1))
@@ -390,7 +390,7 @@ def tile_dwarfattention_pa_kernel(tc, x, W_qkv, b_qkv, gains, pos_bias, identity
                         out=sp[:, sl * P:(sl + 1) * P],
                         lhsT=pt[:, a, :],
                         rhs=ident[:],
-                        is_transpose=(a != 0),
+                        is_transpose=True,
                         start=(a == 0),
                         stop=(a == 7),
                     )
@@ -532,7 +532,7 @@ def tile_dwarfattention_pa_kernel(tc, x, W_qkv, b_qkv, gains, pos_bias, identity
                     )
 
             def do_f2(t):
-                O0[t] = sp2.tile([P, E], F32, name="o0")
+                O0[t] = sp1.tile([P, E], F32, name="o0")
                 nc.vector.tensor_copy(out=O0[t][:, 0:512], in_=BP[t][0][:])
                 nc.scalar.copy(out=O0[t][:, 512:E], in_=BP[t][1][:])
 

@@ -29,25 +29,34 @@ BIG = 3.0e38
 
 FLOPS = 2 * NTOK * 3 * E * DM + 4 * NTOK * E * NOFF
 
-TILE_ORDER = [0, 2, 3, 4, 5, 6, 7, 8, 9, 10, 11, 1]
-SPLIT = {0: (12, 4), 2: (12, 4), 3: (12, 4), 4: (12, 4), 5: (12, 4), 6: (12, 4), 7: (12, 4), 8: (12, 4),
-         9: (12, 4), 10: (12, 4), 11: (8, 4), 1: (8, 4)}
+TILE_ORDER = [11, 10, 9, 8, 7, 6, 5, 4, 3, 2, 1, 0]
+HG = 4
+IW = HG * HD
+WP_BATCHES = [[1, 2, 3, 4], [5, 6, 7], [12, 13, 14, 15], [16, 17, 18]]
+WP_STEP = 112
+TAIL_PATTERN = "SVSVSVSVSVSVSVVS"
 
 C_PRE = 0
 C_RED = 1
 C_SW = 2
 C_QP = 3
 C_M1 = 4
-C_SH = 5
-C_QKT = 6
-C_MUL = 7
-C_ADD = 8
-C_F1 = 9
-C_FIN = 10
+C_WT = 5
+C_WC = 6
+C_QKT = 7
+C_MUL = 8
+C_ADD = 9
+C_F1 = 10
+C_FIN = 11
 
 
 def valid_ids(t):
     return [i for i in range(NOFF) if OFFS[i] < P * (t + 1)]
+
+
+def round_order(t):
+    ids = valid_ids(t)
+    return [i for i in ids if OFFS[i] % P == 0] + [i for i in ids if OFFS[i] % P != 0]
 
 
 def build_plan():
@@ -78,37 +87,48 @@ def build_plan():
         at(last + 8, C_SW, ("sw4", t))
         at(last + 9, C_SW, ("sw5", t))
         at(last + 10, C_SW, ("sw6", t))
-        ready[t] = last + 12
-
-    def place_fin(t, f):
-        at(f, C_SH, ("bt", t))
-        at(f + 1, C_MUL, ("f2", t))
-        at(f + 2, C_FIN, ("f3", t))
-        at(f + 3, C_FIN, ("f4", t))
+        at(last + 11, C_WT, ("wt", t))
+        at(last + 12, C_WC, ("wtc", t))
+        for b in range(len(WP_BATCHES)):
+            at(last + 13 + 2 * b, C_WT, ("wp", t, b))
+            at(last + 14 + 2 * b, C_WC, ("wpc", t, b))
+        ready[t] = last + 17
+    products_end = n
 
     cur = 0
-    pend = []
     for t in TILE_ORDER:
-        ids = valid_ids(t)
-        for k, i in enumerate(ids):
-            step = max(cur, ready[t])
-            if pend and pend[0][1] <= step:
-                f = max(cur, pend[0][1])
-                place_fin(pend[0][0], f)
-                pend = []
-                cur = f + 1
-                step = max(cur, ready[t])
-            first = k == 0
-            last = k == len(ids) - 1
-            if OFFS[i] % P != 0:
-                at(step - 4, C_SH, ("sh", t, i))
-            at(step + 1, C_MUL, ("mul", t, i))
-            at(step + 2, C_ADD, ("add", t, i, first, last))
-            if last:
-                at(step + 2, C_F1, ("f1", t))
-                pend = [(t, step + 3)]
-            cur = step + 1
-    place_fin(pend[0][0], max(cur, pend[0][1]))
+        items = [(hg, i) for hg in range(H // HG) for i in round_order(t)]
+        step = max(cur, ready[t])
+        last_add = {}
+        owe = False
+        for k, (hg, i) in enumerate(items):
+            st = step + k // 4
+            if st >= products_end:
+                eng = TAIL_PATTERN[k % len(TAIL_PATTERN)]
+            else:
+                eng = "S"
+                if k % 4 == 3 or owe:
+                    owe = i == 0
+                    if i != 0:
+                        eng = "G"
+            lat = 3 if eng == "G" else 2
+            at(st + 1, C_MUL, ("mul", t, hg, i, eng))
+            at(st + lat, C_ADD, ("add", t, hg, i))
+            last_add[hg] = max(last_add.get(hg, 0), st + lat)
+        cur = step + (len(items) + 3) // 4
+        for hg in range(H // HG):
+            f = last_add[hg] + 1
+            at(f, C_F1, ("fl", t, hg))
+            if t < NT - 1:
+                at(f, C_F1, ("fr", t, hg))
+                at(f + 1, C_WT, ("bt", t, hg))
+                at(f + 2, C_F1, ("f2", t, hg))
+                if hg == H // HG - 1:
+                    at(f + 3, C_FIN, ("f3", t + 1))
+                    at(f + 4, C_FIN, ("f4", t + 1))
+                    if t == 0:
+                        at(f + 3, C_FIN, ("f3", 0))
+                        at(f + 4, C_FIN, ("f4", 0))
     return plan
 
 
@@ -312,13 +332,18 @@ def tile_dwarfattention_pa_kernel(tc, x, W_qkv, b_qkv, gains, pos_bias, identity
 
         with ExitStack() as p1:
             ptp = p1.enter_context(tc.tile_pool(name="ptp", bufs=3))
-            tmpp = p1.enter_context(tc.tile_pool(name="tmpp", bufs=3))
-            vop = p1.enter_context(tc.tile_pool(name="vop", bufs=6))
+            tmpp = p1.enter_context(tc.tile_pool(name="tmpp", bufs=12))
             sp3 = p1.enter_context(tc.tile_pool(name="sp3", bufs=3))
             sp2 = p1.enter_context(tc.tile_pool(name="sp2", bufs=2))
             sp1 = p1.enter_context(tc.tile_pool(name="sp1", bufs=1))
             sps = p1.enter_context(tc.psum_pool(name="sps", bufs=2))
+            avp = p1.enter_context(tc.psum_pool(name="avp", bufs=2))
             one = p1.enter_context(tc.psum_pool(name="one", bufs=1))
+
+            WT = sp1.tile([P, 2, NTOK + P], F32, name="WT")
+            nc.gpsimd.memset(WT[:, :, NTOK:NTOK + P], 0.0)
+            zero = sp1.tile([P, P], F32, name="zero")
+            nc.gpsimd.memset(zero[:], 0.0)
 
             pos_of = {}
             for k, t in enumerate(TILE_ORDER):
@@ -331,10 +356,12 @@ def tile_dwarfattention_pa_kernel(tc, x, W_qkv, b_qkv, gains, pos_bias, identity
             ZW = {}
             RZ = {}
             W = {}
-            VO = {}
+            WPS = {}
+            WS = {}
             TMP = {}
-            ACC = {}
-            ACS = {}
+            AV = {}
+            LSB = {}
+            RSB = {}
             BP = {}
             O0 = {}
             R = {}
@@ -461,80 +488,110 @@ def tile_dwarfattention_pa_kernel(tc, x, W_qkv, b_qkv, gains, pos_bias, identity
                     op=ALU.mult,
                 )
 
-            def do_sh(t, i):
-                vo = vop.tile([P, E], F32, name="vo")
-                VO[(t, i)] = vo
-                a = OFFS[i] // P
-                r = OFFS[i] % P
-                pieces = [(r, 0, P - r, t - a)]
-                if t - a - 1 >= 0:
-                    pieces.append((0, P - r, r, t - a - 1))
-                else:
-                    nc.gpsimd.memset(vo[0:r, :], 0.0)
-                for (d0, s0, cnt, tile_ix) in pieces:
-                    big = cnt - cnt % 16
-                    for (off, n) in ((0, big), (big, cnt - big)):
-                        if n > 0:
-                            nc.sync.dma_start(
-                                out=vo[d0 + off:d0 + off + n, :], in_=vA[s0 + off:s0 + off + n, tile_ix, :]
-                            )
+            def do_wt(t):
+                wps = one.tile([P, 512], F32, name="wps")
+                WPS[t] = wps
+                for g in range(2):
+                    nc.tensor.transpose(
+                        wps[:, g * P:(g + 1) * P], W[t][:, 12 * g:12 * g + 8, :].rearrange("p a b -> p (a b)"), ident[:]
+                    )
 
-            def do_mul(t, i):
-                hs, hg = SPLIT[t]
-                if OFFS[i] % P != 0:
-                    vo = VO[(t, i)][:]
-                else:
-                    vo = vA[:, t - OFFS[i] // P, :]
-                w = W[t]
-                tmp = tmpp.tile([P, E], F32, name="tmp")
-                TMP[(t, i)] = tmp
-                for (eng, h0, h1) in ((nc.gpsimd, hs, hs + hg), (nc.vector, hs + hg, H)):
-                    if h1 > h0:
-                        eng.tensor_tensor(
-                            out=tmp[:, h0 * HD:h1 * HD].rearrange("p (h d) -> p h d", d=HD),
-                            in0=vo[:, h0 * HD:h1 * HD].rearrange("p (h d) -> p h d", d=HD),
-                            in1=w[:, i, h0:h1].unsqueeze(2).to_broadcast([P, h1 - h0, HD]),
-                            op=ALU.mult,
+            def do_wtc(t):
+                nc.scalar.copy(
+                    out=WT[:, :, t * P:(t + 1) * P], in_=WPS[t][:, 0:2 * P].rearrange("p (g c) -> p g c", g=2)
+                )
+
+            def do_wp(t, b):
+                wps = one.tile([P, 512], F32, name="wps")
+                WPS[t] = wps
+                for k, i in enumerate(WP_BATCHES[b]):
+                    lo = t * P + OFFS[i] % P
+                    nc.tensor.transpose(wps[:, WP_STEP * k:WP_STEP * k + P], WT[:, i // 12, lo:lo + P], ident[:])
+
+            def do_wpc(t, b):
+                ids = WP_BATCHES[b]
+                if b == 0:
+                    WS[t] = sp2.tile([P, NOFF, H], F32, name="ws")
+                c0 = H * (ids[0] % 12)
+                nc.scalar.copy(
+                    out=WS[t][:, ids[0]:ids[0] + len(ids), :],
+                    in_=WPS[t][:, 0:len(ids) * P].rearrange("p (k c) -> p k c", c=P)[:, :, c0:c0 + H],
+                )
+
+            def do_mul(t, hg, i, eng):
+                src = vA[:, t - OFFS[i] // P, hg * IW:(hg + 1) * IW]
+                w = W[t] if OFFS[i] % P == 0 else WS[t]
+                tmp = tmpp.tile([P, IW], F32, name="tmp")
+                TMP[(t, hg, i)] = tmp
+                if eng == "S":
+                    for hh in range(HG):
+                        cols = slice(hh * HD, (hh + 1) * HD)
+                        nc.scalar.activation(
+                            out=tmp[:, cols], in_=src[:, cols], func=ACT.Copy, scale=w[:, i, hg * HG + hh:hg * HG + hh + 1]
                         )
-                for h in range(hs):
-                    cols = slice(h * HD, (h + 1) * HD)
-                    nc.scalar.activation(out=tmp[:, cols], in_=vo[:, cols], func=ACT.Copy, scale=w[:, i, h:h + 1])
+                else:
+                    engine = nc.gpsimd if eng == "G" else nc.vector
+                    engine.tensor_tensor(
+                        out=tmp[:].rearrange("p (h d) -> p h d", d=HD),
+                        in0=src.rearrange("p (h d) -> p h d", d=HD),
+                        in1=w[:, i, hg * HG:(hg + 1) * HG].unsqueeze(2).to_broadcast([P, HG, HD]),
+                        op=ALU.mult,
+                    )
 
-            def do_add(t, i, first, last):
+            def do_add(t, hg, i, first, last):
                 if first:
-                    acc0 = one.tile([P, 512], F32, name="acc0")
-                    acc1 = one.tile([P, 512], F32, name="acc1")
-                    ACC[t] = (acc0, acc1)
-                tmp = TMP[(t, i)]
-                for ft in range(8):
+                    AV[(t, hg)] = avp.tile([P, 2, 2 * P], F32, name="av")
+                av = AV[(t, hg)]
+                tmp = TMP[(t, hg, i)]
+                r = OFFS[i] % P
+                for ftl in range(2):
                     nc.tensor.matmul(
-                        out=ACC[t][ft // 4][:, (ft % 4) * P:(ft % 4 + 1) * P],
-                        lhsT=tmp[:, ft * P:(ft + 1) * P],
+                        out=av[:, ftl, r:r + P],
+                        lhsT=tmp[:, ftl * P:(ftl + 1) * P],
                         rhs=ident[:],
                         is_transpose=True,
-                        start=(first and ft % 4 == 0),
-                        stop=(last and ft % 4 == 3),
+                        start=(first and ftl == 0),
+                        stop=(last and ftl == 1),
+                    )
+                if first:
+                    for ftl in range(2):
+                        nc.tensor.matmul(
+                            out=av[:, ftl, P:2 * P], lhsT=zero[:], rhs=ident[:], is_transpose=True, start=False, stop=False
+                        )
+
+            def do_fl(t, hg):
+                if hg == 0:
+                    LSB[t] = sp2.tile([P, 8, P], F32, name="lsb")
+                nc.scalar.copy(out=LSB[t][:, 2 * hg:2 * hg + 2, :], in_=AV[(t, hg)][:, :, 0:P])
+
+            def do_fr(t, hg):
+                RSB[(t, hg)] = sp2.tile([P, 2, P], F32, name="rsb")
+                nc.scalar.copy(out=RSB[(t, hg)][:], in_=AV[(t, hg)][:, :, P:2 * P])
+
+            def do_bt(t, hg):
+                bp = one.tile([P, 512], F32, name="bp")
+                BP[t] = bp
+                seq = []
+                for ftl in range(2):
+                    seq.append((ftl, LSB[t + 1][:, 2 * hg + ftl, :]))
+                    seq.append((ftl, RSB[(t, hg)][:, ftl, :]))
+                if t == 0:
+                    for ftl in range(2):
+                        seq.append((2 + ftl, LSB[0][:, 2 * hg + ftl, :]))
+                for k, (blk, ap) in enumerate(seq):
+                    nc.tensor.matmul(
+                        out=bp[:, blk * P:(blk + 1) * P], lhsT=ap, rhs=ident[:], is_transpose=True,
+                        start=(k == 0), stop=(k == len(seq) - 1),
                     )
 
-            def do_f1(t):
-                acs = sp1.tile([P, E], F32, name="acs")
-                ACS[t] = acs
-                nc.vector.tensor_copy(out=acs[:, 0:512], in_=ACC[t][0][:])
-                nc.scalar.copy(out=acs[:, 512:E], in_=ACC[t][1][:])
-
-            def do_bt(t):
-                bp0 = one.tile([P, 512], F32, name="bp0")
-                bp1 = one.tile([P, 512], F32, name="bp1")
-                BP[t] = (bp0, bp1)
-                for ft in range(8):
-                    nc.tensor.transpose(
-                        BP[t][ft // 4][:, (ft % 4) * P:(ft % 4 + 1) * P], ACS[t][:, ft * P:(ft + 1) * P], ident[:]
-                    )
-
-            def do_f2(t):
-                O0[t] = sp1.tile([P, E], F32, name="o0")
-                nc.vector.tensor_copy(out=O0[t][:, 0:512], in_=BP[t][0][:])
-                nc.scalar.copy(out=O0[t][:, 512:E], in_=BP[t][1][:])
+            def do_f2(t, hg):
+                if hg == 0:
+                    O0[t + 1] = sp2.tile([P, E], F32, name="o0")
+                    if t == 0:
+                        O0[0] = sp2.tile([P, E], F32, name="o0")
+                nc.scalar.copy(out=O0[t + 1][:, hg * IW:(hg + 1) * IW], in_=BP[t][:, 0:IW])
+                if t == 0:
+                    nc.vector.tensor_copy(out=O0[0][:, hg * IW:(hg + 1) * IW], in_=BP[t][:, IW:2 * IW])
 
             def do_f3(t):
                 am = sp2.tile([P, 1], F32, name="am")
@@ -554,11 +611,25 @@ def tile_dwarfattention_pa_kernel(tc, x, W_qkv, b_qkv, gains, pos_bias, identity
 
             table = {
                 "pre": do_pre, "qp": do_qp, "m1": do_m1, "qkt": do_qkt, "red": do_red, "sw1": do_sw1,
-                "sw2": do_sw2, "sw3": do_sw3, "sw4": do_sw4, "sw5": do_sw5, "sw6": do_sw6, "sh": do_sh,
-                "mul": do_mul, "add": do_add, "f1": do_f1, "bt": do_bt, "f2": do_f2, "f3": do_f3, "f4": do_f4,
+                "sw2": do_sw2, "sw3": do_sw3, "sw4": do_sw4, "sw5": do_sw5, "sw6": do_sw6, "wt": do_wt,
+                "wtc": do_wtc, "wp": do_wp, "wpc": do_wpc, "mul": do_mul, "add": do_add, "fl": do_fl, "fr": do_fr,
+                "bt": do_bt, "f2": do_f2, "f3": do_f3, "f4": do_f4,
             }
             plan = build_plan()
+            items = []
+            for key in sorted(plan.keys()):
+                items.extend(plan[key])
+            first_add = {}
+            last_add = {}
+            for k, item in enumerate(items):
+                if item[0] == "add":
+                    first_add.setdefault((item[1], item[2]), k)
+                    last_add[(item[1], item[2])] = k
             with tc.manual_schedule():
-                for key in sorted(plan.keys()):
-                    for item in plan[key]:
+                for k, item in enumerate(items):
+                    if item[0] == "add":
+                        grp = (item[1], item[2])
+                        assert first_add[grp] != k or item[3] == 0
+                        do_add(item[1], item[2], item[3], first_add[grp] == k, last_add[grp] == k)
+                    else:
                         table[item[0]](*item[1:])

from contextlib import ExitStack

import concourse.mybir as mybir
from concourse.masks import make_identity

F32 = mybir.dt.float32
BF16 = mybir.dt.bfloat16
U32 = mybir.dt.uint32
U8 = mybir.dt.uint8
FP8X4 = mybir.dt.float8_e4m3fn_x4
FP8 = mybir.dt.float8_e4m3fn
ALU = mybir.AluOpType
ACT = mybir.ActivationFunctionType
AX = mybir.AxisListType

P = 128
NTOK = 1536
NT = 12
DM = 1024
E = 1024
H = 16
HD = 64
PAD = 128
D4 = [0.4829629131445341, 0.8365163037378079, 0.2241438680420134, -0.1294095225512604]
OFFS = [0, 1, 2, 4, 8, 16, 32, 64, 128, 256, 512, 1024, 3, 6, 12, 24, 48, 96, 192, 384, 768]
NOFF = 21
NSLOT = 43
BIG = 3.0e38

FLOPS = 2 * NTOK * 3 * E * DM + 4 * NTOK * E * NOFF

TILE_ORDER = [11, 10, 9, 8, 7, 6, 5, 4, 3, 2, 1, 0]
HG = 4
IW = HG * HD
WP_BATCHES = [[1, 2, 3, 4], [5, 6, 7], [12, 13, 14, 15], [16, 17, 18]]
WP_STEP = 112
TAIL_PATTERN = "SVSVSVSVSVSVSVVS"

C_PRE = 0
C_RED = 1
C_SW = 2
C_QP = 3
C_M1 = 4
C_WT = 5
C_WC = 6
C_QKT = 7
C_MUL = 8
C_ADD = 9
C_F1 = 10
C_FIN = 11


def valid_ids(t):
    return [i for i in range(NOFF) if OFFS[i] < P * (t + 1)]


def round_order(t):
    ids = valid_ids(t)
    return [i for i in ids if OFFS[i] % P == 0] + [i for i in ids if OFFS[i] % P != 0]


def build_plan():
    plan = {}

    def at(step, cls, item):
        plan.setdefault((step, cls), []).append(item)

    ready = {}
    n = 0
    for t in TILE_ORDER:
        ids = valid_ids(t)
        at(n, C_PRE, ("pre", t))
        at(n, C_QP, ("qp", t))
        for grp in ([i for i in ids if i < 12], [i for i in ids if i >= 12]):
            for c0 in range(0, len(grp), 4):
                ch = grp[c0:c0 + 4]
                for sl, i in enumerate(ch):
                    at(n, C_M1, ("m1", t, i))
                    at(n + 1, C_QKT, ("qkt", t, i, sl))
                    if sl == len(ch) - 1:
                        at(n + 2, C_RED, ("red", t, ch[0], len(ch)))
                    n += 1
        last = n - 1
        at(last + 2, C_SW, ("sw1", t))
        at(last + 4, C_SW, ("sw2", t))
        at(last + 6, C_SW, ("sw3", t))
        at(last + 8, C_SW, ("sw4", t))
        at(last + 9, C_SW, ("sw5", t))
        at(last + 10, C_SW, ("sw6", t))
        at(last + 11, C_WT, ("wt", t))
        at(last + 12, C_WC, ("wtc", t))
        for b in range(len(WP_BATCHES)):
            at(last + 13 + 2 * b, C_WT, ("wp", t, b))
            at(last + 14 + 2 * b, C_WC, ("wpc", t, b))
        ready[t] = last + 17
    products_end = n

    cur = 0
    for t in TILE_ORDER:
        items = [(hg, i) for hg in range(H // HG) for i in round_order(t)]
        step = max(cur, ready[t])
        last_add = {}
        owe = False
        for k, (hg, i) in enumerate(items):
            st = step + k // 4
            if st >= products_end:
                eng = TAIL_PATTERN[k % len(TAIL_PATTERN)]
            else:
                eng = "S"
                if k % 4 == 3 or owe:
                    owe = i == 0
                    if i != 0:
                        eng = "G"
            lat = 3 if eng == "G" else 2
            at(st + 1, C_MUL, ("mul", t, hg, i, eng))
            at(st + lat, C_ADD, ("add", t, hg, i))
            last_add[hg] = max(last_add.get(hg, 0), st + lat)
        cur = step + (len(items) + 3) // 4
        for hg in range(H // HG):
            f = last_add[hg] + 1
            at(f, C_F1, ("fl", t, hg))
            if t < NT - 1:
                at(f, C_F1, ("fr", t, hg))
                at(f + 1, C_WT, ("bt", t, hg))
                at(f + 2, C_F1, ("f2", t, hg))
                if hg == H // HG - 1:
                    at(f + 3, C_FIN, ("f3", t + 1))
                    at(f + 4, C_FIN, ("f4", t + 1))
                    if t == 0:
                        at(f + 3, C_FIN, ("f3", 0))
                        at(f + 4, C_FIN, ("f4", 0))
    return plan


def tile_dwarfattention_pa_kernel(tc, x, W_qkv, b_qkv, gains, pos_bias, identity_bypass, out_0, out_1):
    nc = tc.nc
    x2 = x.flatten_outer_dims()
    o0_dram = out_0.flatten_outer_dims()
    o1_dram = out_1.flatten_outer_dims()

    with ExitStack() as ctx:
        keep = ctx.enter_context(tc.tile_pool(name="keep", bufs=1))

        ident = keep.tile([P, P], F32, name="ident")
        make_identity(nc, ident[:])

        qA = keep.tile([P, NT, E], F32, name="qA")
        kT = keep.tile([P, 8, PAD + NTOK], F32, name="kT")
        vA = keep.tile([P, NT, E], F32, name="vA")
        graw = keep.tile([P, 11, H, NT], BF16, name="graw")
        bk = keep.tile([P, 8], F32, name="bk")
        biasB = keep.tile([P, NSLOT, H], F32, name="biasB")
        gw_tiles = [keep.tile([P, NSLOT, H], F32, name="gw0"), keep.tile([P, NSLOT, H], F32, name="gw1")]
        nc.gpsimd.memset(kT[:, :, 0:PAD], 0.0)

        with ExitStack() as p0:
            rawp = p0.enter_context(tc.tile_pool(name="rawp", bufs=4))
            xgp = p0.enter_context(tc.tile_pool(name="xgp", bufs=2))
            wgp = p0.enter_context(tc.tile_pool(name="wgp", bufs=2))
            wcp = p0.enter_context(tc.tile_pool(name="wcp", bufs=4))
            mvp = p0.enter_context(tc.tile_pool(name="mvp", bufs=2))
            cod = p0.enter_context(tc.tile_pool(name="cod", bufs=1))
            pst = p0.enter_context(tc.psum_pool(name="pst", bufs=3))
            psm = p0.enter_context(tc.psum_pool(name="psm", bufs=4))

            bkraw = cod.tile([P, 8], BF16, name="bkraw")
            pbraw = cod.tile([P, 44 * H], BF16, name="pbraw")
            ibraw = cod.tile([P, H], BF16, name="ibraw")
            nc.scalar.dma_start(out=bkraw[:], in_=b_qkv[E:2 * E].rearrange("(j a) -> j a", a=8))
            nc.scalar.dma_start(out=pbraw[:], in_=pos_bias.rearrange("r h -> (r h)").partition_broadcast(P))
            nc.scalar.dma_start(out=ibraw[:], in_=identity_bypass.partition_broadcast(P))
            identb = cod.tile([P, P], BF16, name="identb")
            make_identity(nc, identb[:])
            gr = [cod.tile([P, P * 11], BF16, name="gr0"), cod.tile([P, P * 11], BF16, name="gr1")]
            for half in range(2):
                nc.gpsimd.memset(gr[half][96:P, :], 0.0)
                nc.scalar.dma_start(
                    out=gr[half][0:96, :],
                    in_=gains[0, 8 * half:8 * half + 8, :, :].rearrange("h (t n) j -> (h t) (n j)", t=NT),
                )
            graw_q = graw[:].rearrange("p j h t -> p (j h t)").rearrange("p (q c) -> p q c", c=96)
            for q0 in range(0, 22, 4):
                nq = min(4, 22 - q0)
                gp = pst.tile([P, 4, P], BF16, name="tp")
                for k in range(nq):
                    nc.tensor.transpose(gp[:, k, :], gr[(q0 + k) % 2][:, (q0 + k) // 2:P * 11:11], identb[:])
                nc.vector.tensor_copy(out=graw_q[:, q0:q0 + nq, :], in_=gp[:, 0:nq, 0:96])

            nc.vector.tensor_copy(out=bk[:], in_=bkraw[:])

            pb4 = pbraw[:].rearrange("p (j c h) -> p j c h", c=4, h=H)
            nc.vector.memset(biasB[:, 11:13, :], 0.0)
            nc.vector.tensor_copy(out=biasB[:, 0:11, :], in_=pb4[:, :, 0, :])
            nc.vector.tensor_copy(out=biasB[:, 13:23, :], in_=pb4[:, 0:10, 2, :])
            nc.vector.tensor_copy(out=biasB[:, 23:34, :], in_=pb4[:, :, 1, :])
            nc.vector.tensor_copy(out=biasB[:, 34:43, :], in_=pb4[:, 0:9, 3, :])

            ib = cod.tile([P, H], F32, name="ib")
            sp_a = cod.tile([P, H], F32, name="sp_a")
            nc.vector.tensor_copy(out=ib[:], in_=ibraw[:])
            nc.scalar.activation(out=sp_a[:], in_=ib[:], func=ACT.Abs)
            nc.scalar.activation(out=sp_a[:], in_=sp_a[:], func=ACT.Exp, scale=-1.0)
            nc.vector.tensor_scalar(out=sp_a[:], in0=sp_a[:], scalar1=1.0, scalar2=None, op0=ALU.add)
            nc.scalar.activation(out=sp_a[:], in_=sp_a[:], func=ACT.Ln)
            for gw in gw_tiles:
                nc.vector.memset(gw[:, 12, :], 0.0)
                nc.vector.scalar_tensor_tensor(
                    out=gw[:, 11, :], in0=ib[:], scalar=0.0, in1=sp_a[:], op0=ALU.max, op1=ALU.add
                )

            xc = cod.tile([P, 2, NTOK], U32, name="xc", align_bytes=64)
            xs = cod.tile([P, 2, NTOK], U8, name="xs", align_bytes=64)

            bqB = cod.tile([P, E], F32, name="bqB")
            bvB = cod.tile([P, E], F32, name="bvB")
            bq_raw = rawp.tile([P, DM], BF16, name="raw")
            nc.scalar.dma_start(out=bq_raw[:], in_=b_qkv[0:E].partition_broadcast(P))
            nc.gpsimd.tensor_copy(
                out=bqB[:].rearrange("p (a j) -> p a j", a=8), in_=bq_raw[:].rearrange("p (j a) -> p a j", a=8)
            )
            bv_raw = rawp.tile([P, DM], BF16, name="raw")
            nc.scalar.dma_start(out=bv_raw[:], in_=b_qkv[2 * E:3 * E].partition_broadcast(P))
            nc.gpsimd.tensor_copy(out=bvB[:], in_=bv_raw[:])

            def turn(rows, dst_words):
                raw = rawp.tile([P, DM], BF16, name="raw")
                nc.sync.dma_start(out=raw[:], in_=rows)
                words = raw[:].bitcast(F32)
                tp = pst.tile([P, 2, 2, P], F32, name="tp")
                for g in range(2):
                    for u in range(2):
                        nc.tensor.transpose(tp[:, g, u, :], words[:, 256 * g + u:256 * (g + 1):2], ident[:])
                nc.scalar.copy(out=dst_words, in_=tp[:].rearrange("p g u r -> p g r u"))

            def quantize_512(row_blocks, cd, sc):
                xg = xgp.tile([P, 2, 512, 4], BF16, name="xg", align_bytes=64)
                for r in range(4):
                    turn(row_blocks[r], xg[:, :, r * P:(r + 1) * P, :].bitcast(F32))
                for g in range(2):
                    nc.vector.quantize_mx(
                        out=cd[g].bitcast(FP8X4), scales=sc[g], in_=xg[:, g, :, :].rearrange("p r j -> p (r j)")
                    )

            for c in range(3):
                cols = slice(c * 512, (c + 1) * 512)
                quantize_512(
                    [x2[c * 512 + r * P:c * 512 + (r + 1) * P, :] for r in range(4)],
                    [xc[:, g, cols] for g in range(2)],
                    [xs[:, g, cols] for g in range(2)],
                )

            wq_view = W_qkv[0:E, :].rearrange("(j a) k -> a j k", a=8)
            wk_view = W_qkv[E:2 * E, :].rearrange("(j a) k -> a j k", a=8)
            codes = {}

            def prep_k(a):
                wg = wgp.tile([P, 2, P, 4], BF16, name="wg", align_bytes=64)
                turn(wk_view[a], wg[:].bitcast(F32))
                wc = wcp.tile([P, 2 * P], U32, name="wc", align_bytes=64)
                ws = wcp.tile([P, 2 * P], U8, name="ws", align_bytes=64)
                nc.vector.quantize_mx(
                    out=wc[:].bitcast(FP8X4), scales=ws[:], in_=wg[:].rearrange("p g r j -> p (g r j)")
                )
                codes[a] = (wc, ws)

            def project_k(a):
                wc, ws = codes[a]
                for c in range(3):
                    cols = slice(c * 512, (c + 1) * 512)
                    acc = psm.tile([P, 512], F32, name="acc")
                    for g in range(2):
                        nc.tensor.matmul_mx(
                            out=acc[:],
                            lhsT=wc[:, g * P:(g + 1) * P].bitcast(FP8X4),
                            lhsT_scale=ws[:, g * P:(g + 1) * P],
                            rhs=xc[:, g, cols].bitcast(FP8X4),
                            rhs_scale=xs[:, g, cols],
                            start=(g == 0),
                            stop=(g == 1),
                        )
                    nc.scalar.activation(
                        out=kT[:, a, PAD + c * 512:PAD + (c + 1) * 512], in_=acc[:], func=ACT.Identity,
                        bias=bk[:, a:a + 1], scale=1.0,
                    )

            def prep_moving(key, row_blocks):
                mc = mvp.tile([P, 2, 512], U32, name="mc", align_bytes=64)
                ms = mvp.tile([P, 2, 512], U8, name="ms", align_bytes=64)
                quantize_512(row_blocks, [mc[:, g, :] for g in range(2)], [ms[:, g, :] for g in range(2)])
                codes[key] = (mc, ms)

            def project_tokens(key, dst, bias_row, c):
                mc, ms = codes[key]
                cols = slice(c * 512, (c + 1) * 512)
                for tt in range(NT):
                    acc = psm.tile([P, 512], F32, name="acc")
                    for g in range(2):
                        nc.tensor.matmul_mx(
                            out=acc[:],
                            lhsT=xc[:, g, tt * P:(tt + 1) * P].bitcast(FP8X4),
                            lhsT_scale=xs[:, g, tt * P:(tt + 1) * P],
                            rhs=mc[:, g, :].bitcast(FP8X4),
                            rhs_scale=ms[:, g, :],
                            start=(g == 0),
                            stop=(g == 1),
                        )
                    nc.vector.tensor_tensor(out=dst[:, tt, cols], in0=acc[:], in1=bias_row[:, cols], op=ALU.add)

            def q_blocks(c):
                return [wq_view[4 * c + r] for r in range(4)]

            def v_blocks(c):
                return [W_qkv[2 * E + c * 512 + r * P:2 * E + c * 512 + (r + 1) * P, :] for r in range(4)]

            prep_k(0)
            prep_k(1)
            for a0 in range(0, 8, 2):
                if a0 + 2 < 8:
                    prep_k(a0 + 2)
                    prep_k(a0 + 3)
                else:
                    prep_moving("q0", q_blocks(0))
                project_k(a0)
                project_k(a0 + 1)
            prep_moving("q1", q_blocks(1))
            project_tokens("q0", qA, bqB, 0)
            prep_moving("v0", v_blocks(0))
            project_tokens("q1", qA, bqB, 1)
            prep_moving("v1", v_blocks(1))
            project_tokens("v0", vA, bvB, 0)
            project_tokens("v1", vA, bvB, 1)

        with ExitStack() as p1:
            ptp = p1.enter_context(tc.tile_pool(name="ptp", bufs=3))
            tmpp = p1.enter_context(tc.tile_pool(name="tmpp", bufs=12))
            sp3 = p1.enter_context(tc.tile_pool(name="sp3", bufs=3))
            sp2 = p1.enter_context(tc.tile_pool(name="sp2", bufs=2))
            sp1 = p1.enter_context(tc.tile_pool(name="sp1", bufs=1))
            sps = p1.enter_context(tc.psum_pool(name="sps", bufs=2))
            avp = p1.enter_context(tc.psum_pool(name="avp", bufs=2))
            one = p1.enter_context(tc.psum_pool(name="one", bufs=1))

            WT = sp1.tile([P, 2, NTOK + P], F32, name="WT")
            nc.gpsimd.memset(WT[:, :, NTOK:NTOK + P], 0.0)
            zero = sp1.tile([P, P], F32, name="zero")
            nc.gpsimd.memset(zero[:], 0.0)

            pos_of = {}
            for k, t in enumerate(TILE_ORDER):
                pos_of[t] = k
            S = {}
            QP = {}
            PT = {}
            SP = {}
            UE = {}
            ZW = {}
            RZ = {}
            W = {}
            WPS = {}
            WS = {}
            TMP = {}
            AV = {}
            LSB = {}
            RSB = {}
            BP = {}
            O0 = {}
            R = {}

            def win(t, i):
                lo = PAD + t * P - OFFS[i]
                return slice(lo, lo + P)

            def do_pre(t):
                s = sp2.tile([P, NOFF, H], F32, name="s")
                S[t] = s
                ids = valid_ids(t)
                na = len([i for i in ids if i < 12])
                nb = len(ids) - na
                if na < 12:
                    nc.gpsimd.memset(s[:, na:12, :], 0.0)
                if nb < 9:
                    nc.gpsimd.memset(s[:, 12 + nb:NOFF, :], 0.0)
                gw = gw_tiles[pos_of[t] % 2]
                for (lo, nj, c) in ((0, 11, D4[0]), (13, 10, D4[2]), (23, 11, D4[1]), (34, 9, -D4[3])):
                    nc.gpsimd.tensor_scalar(
                        out=gw[:, lo:lo + nj, :],
                        in0=graw[:, 0:nj, :, t],
                        scalar1=c,
                        scalar2=0.0,
                        op0=ALU.mult,
                        op1=ALU.add,
                    )

            def do_qp(t):
                qp0 = one.tile([P, 4, P], F32, name="qp0")
                qp1 = one.tile([P, 4, P], F32, name="qp1")
                QP[t] = (qp0, qp1)
                for a in range(8):
                    nc.tensor.transpose(QP[t][a // 4][:, a % 4, :], qA[:, t, a * P:(a + 1) * P], ident[:])

            def do_m1(t, i):
                pt = ptp.tile([P, 8, P], F32, name="pt")
                PT[(t, i)] = pt
                for b in range(2):
                    nc.vector.tensor_tensor(
                        out=pt[:, 4 * b:4 * b + 4, :], in0=QP[t][b][:], in1=kT[:, 4 * b:4 * b + 4, win(t, i)],
                        op=ALU.mult,
                    )

            def do_qkt(t, i, sl):
                if sl == 0:
                    SP[t] = sps.tile([P, 512], F32, name="sp")
                sp = SP[t]
                pt = PT[(t, i)]
                for a in range(8):
                    nc.tensor.matmul(
                        out=sp[:, sl * P:(sl + 1) * P],
                        lhsT=pt[:, a, :],
                        rhs=ident[:],
                        is_transpose=True,
                        start=(a == 0),
                        stop=(a == 7),
                    )

            def do_red(t, i0, n):
                nc.vector.tensor_reduce(
                    out=S[t][:, i0:i0 + n, :].rearrange("p a b -> p (a b)"),
                    in_=SP[t][:, 0:n * P].rearrange("p (x l) -> p x l", l=8),
                    axis=AX.X,
                    op=ALU.add,
                )

            def do_sw1(t):
                s = S[t]
                u = sp1.tile([P, NSLOT, H], F32, name="u")
                e = sp1.tile([P, NSLOT, H], F32, name="e")
                r = sp1.tile([P, NSLOT, H], F32, name="r")
                UE[t] = (u, e, r)
                nc.gpsimd.tensor_tensor(
                    out=u[:, 0:12, :], in0=s[:, 0:1, :].to_broadcast([P, 12, H]), in1=biasB[:, 0:12, :], op=ALU.add
                )
                nc.gpsimd.tensor_tensor(out=u[:, 12:23, :], in0=s[:, 1:12, :], in1=biasB[:, 12:23, :], op=ALU.add)
                nc.gpsimd.tensor_tensor(out=u[:, 23:43, :], in0=s[:, 1:21, :], in1=biasB[:, 23:43, :], op=ALU.add)
                nc.gpsimd.tensor_scalar(out=r[:], in0=u[:], scalar1=BIG, scalar2=0.0, op0=ALU.min, op1=ALU.max)

            def do_sw2(t):
                u, e, r = UE[t]
                nc.scalar.activation(out=e[:], in_=u[:], func=ACT.Relu, scale=-1.0)
                nc.scalar.activation(out=e[:], in_=e[:], func=ACT.Exp, scale=-1.0)

            def do_sw3(t):
                u, e, r = UE[t]
                gw = gw_tiles[pos_of[t] % 2]
                nc.gpsimd.tensor_tensor(out=r[:], in0=r[:], in1=e[:], op=ALU.add)
                nc.gpsimd.tensor_tensor(out=e[:], in0=r[:], in1=gw[:], op=ALU.mult)

            def do_sw4(t):
                u, e, r = UE[t]
                z = sp2.tile([P, H], F32, name="z")
                wr = sp2.tile([P, 12, H], F32, name="wr")
                ZW[t] = (z, wr)
                nc.vector.tensor_reduce(out=z[:], in_=e[:].rearrange("p s h -> p h s"), axis=AX.X, op=ALU.add)
                nc.vector.tensor_reduce(
                    out=wr[:, 0, :], in_=e[:, 0:12, :].rearrange("p s h -> p h s"), axis=AX.X, op=ALU.add
                )
                nc.gpsimd.tensor_tensor(out=wr[:, 1:12, :], in0=e[:, 12:23, :], in1=e[:, 23:34, :], op=ALU.add)

            def do_sw5(t):
                z, wr = ZW[t]
                rz = sp2.tile([P, H], F32, name="rz")
                nrz = sp2.tile([P, H], F32, name="nrz")
                RZ[t] = (rz, nrz)
                nc.vector.tensor_scalar(out=z[:], in0=z[:], scalar1=1e-6, scalar2=None, op0=ALU.add)
                nc.vector.reciprocal(out=rz[:], in_=z[:])
                nc.vector.tensor_scalar(out=nrz[:], in0=rz[:], scalar1=-1.0, scalar2=None, op0=ALU.mult)

            def do_sw6(t):
                u, e, r = UE[t]
                z, wr = ZW[t]
                rz, nrz = RZ[t]
                w = sp3.tile([P, NOFF, H], F32, name="w")
                W[t] = w
                nc.gpsimd.tensor_tensor(
                    out=w[:, 0:12, :], in0=wr[:], in1=rz[:].unsqueeze(1).to_broadcast([P, 12, H]), op=ALU.mult
                )
                nc.gpsimd.tensor_tensor(
                    out=w[:, 12:21, :], in0=e[:, 34:43, :], in1=nrz[:].unsqueeze(1).to_broadcast([P, 9, H]),
                    op=ALU.mult,
                )

            def do_wt(t):
                wps = one.tile([P, 512], F32, name="wps")
                WPS[t] = wps
                for g in range(2):
                    nc.tensor.transpose(
                        wps[:, g * P:(g + 1) * P], W[t][:, 12 * g:12 * g + 8, :].rearrange("p a b -> p (a b)"), ident[:]
                    )

            def do_wtc(t):
                nc.scalar.copy(
                    out=WT[:, :, t * P:(t + 1) * P], in_=WPS[t][:, 0:2 * P].rearrange("p (g c) -> p g c", g=2)
                )

            def do_wp(t, b):
                wps = one.tile([P, 512], F32, name="wps")
                WPS[t] = wps
                for k, i in enumerate(WP_BATCHES[b]):
                    lo = t * P + OFFS[i] % P
                    nc.tensor.transpose(wps[:, WP_STEP * k:WP_STEP * k + P], WT[:, i // 12, lo:lo + P], ident[:])

            def do_wpc(t, b):
                ids = WP_BATCHES[b]
                if b == 0:
                    WS[t] = sp2.tile([P, NOFF, H], F32, name="ws")
                c0 = H * (ids[0] % 12)
                nc.scalar.copy(
                    out=WS[t][:, ids[0]:ids[0] + len(ids), :],
                    in_=WPS[t][:, 0:len(ids) * P].rearrange("p (k c) -> p k c", c=P)[:, :, c0:c0 + H],
                )

            def do_mul(t, hg, i, eng):
                src = vA[:, t - OFFS[i] // P, hg * IW:(hg + 1) * IW]
                w = W[t] if OFFS[i] % P == 0 else WS[t]
                tmp = tmpp.tile([P, IW], F32, name="tmp")
                TMP[(t, hg, i)] = tmp
                if eng == "S":
                    for hh in range(HG):
                        cols = slice(hh * HD, (hh + 1) * HD)
                        nc.scalar.activation(
                            out=tmp[:, cols], in_=src[:, cols], func=ACT.Copy, scale=w[:, i, hg * HG + hh:hg * HG + hh + 1]
                        )
                else:
                    engine = nc.gpsimd if eng == "G" else nc.vector
                    engine.tensor_tensor(
                        out=tmp[:].rearrange("p (h d) -> p h d", d=HD),
                        in0=src.rearrange("p (h d) -> p h d", d=HD),
                        in1=w[:, i, hg * HG:(hg + 1) * HG].unsqueeze(2).to_broadcast([P, HG, HD]),
                        op=ALU.mult,
                    )

            def do_add(t, hg, i, first, last):
                if first:
                    AV[(t, hg)] = avp.tile([P, 2, 2 * P], F32, name="av")
                av = AV[(t, hg)]
                tmp = TMP[(t, hg, i)]
                r = OFFS[i] % P
                for ftl in range(2):
                    nc.tensor.matmul(
                        out=av[:, ftl, r:r + P],
                        lhsT=tmp[:, ftl * P:(ftl + 1) * P],
                        rhs=ident[:],
                        is_transpose=True,
                        start=(first and ftl == 0),
                        stop=(last and ftl == 1),
                    )
                if first:
                    for ftl in range(2):
                        nc.tensor.matmul(
                            out=av[:, ftl, P:2 * P], lhsT=zero[:], rhs=ident[:], is_transpose=True, start=False, stop=False
                        )

            def do_fl(t, hg):
                if hg == 0:
                    LSB[t] = sp2.tile([P, 8, P], F32, name="lsb")
                nc.scalar.copy(out=LSB[t][:, 2 * hg:2 * hg + 2, :], in_=AV[(t, hg)][:, :, 0:P])

            def do_fr(t, hg):
                RSB[(t, hg)] = sp2.tile([P, 2, P], F32, name="rsb")
                nc.scalar.copy(out=RSB[(t, hg)][:], in_=AV[(t, hg)][:, :, P:2 * P])

            def do_bt(t, hg):
                bp = one.tile([P, 512], F32, name="bp")
                BP[t] = bp
                seq = []
                for ftl in range(2):
                    seq.append((ftl, LSB[t + 1][:, 2 * hg + ftl, :]))
                    seq.append((ftl, RSB[(t, hg)][:, ftl, :]))
                if t == 0:
                    for ftl in range(2):
                        seq.append((2 + ftl, LSB[0][:, 2 * hg + ftl, :]))
                for k, (blk, ap) in enumerate(seq):
                    nc.tensor.matmul(
                        out=bp[:, blk * P:(blk + 1) * P], lhsT=ap, rhs=ident[:], is_transpose=True,
                        start=(k == 0), stop=(k == len(seq) - 1),
                    )

            def do_f2(t, hg):
                if hg == 0:
                    O0[t + 1] = sp2.tile([P, E], F32, name="o0")
                    if t == 0:
                        O0[0] = sp2.tile([P, E], F32, name="o0")
                nc.scalar.copy(out=O0[t + 1][:, hg * IW:(hg + 1) * IW], in_=BP[t][:, 0:IW])
                if t == 0:
                    nc.vector.tensor_copy(out=O0[0][:, hg * IW:(hg + 1) * IW], in_=BP[t][:, IW:2 * IW])

            def do_f3(t):
                am = sp2.tile([P, 1], F32, name="am")
                r = sp2.tile([P, 1], F32, name="r448")
                R[t] = r
                nc.vector.tensor_reduce(out=am[:], in_=O0[t][:], axis=AX.X, op=ALU.max, apply_absolute_value=True)
                nc.vector.reciprocal(out=r[:], in_=am[:])
                nc.vector.tensor_scalar(out=r[:], in0=r[:], scalar1=448.0, scalar2=None, op0=ALU.mult)
                nc.sync.dma_start(out=o0_dram[t * P:(t + 1) * P, :], in_=O0[t][:])

            def do_f4(t):
                o1 = sp2.tile([P, E], FP8, name="o1")
                nc.vector.tensor_scalar(
                    out=o1[:], in0=O0[t][:], scalar1=R[t][:, 0:1], scalar2=None, op0=ALU.mult, saturate=False
                )
                nc.sync.dma_start(out=o1_dram[t * P:(t + 1) * P, :], in_=o1[:].bitcast(U8))

            table = {
                "pre": do_pre, "qp": do_qp, "m1": do_m1, "qkt": do_qkt, "red": do_red, "sw1": do_sw1,
                "sw2": do_sw2, "sw3": do_sw3, "sw4": do_sw4, "sw5": do_sw5, "sw6": do_sw6, "wt": do_wt,
                "wtc": do_wtc, "wp": do_wp, "wpc": do_wpc, "mul": do_mul, "add": do_add, "fl": do_fl, "fr": do_fr,
                "bt": do_bt, "f2": do_f2, "f3": do_f3, "f4": do_f4,
            }
            plan = build_plan()
            items = []
            for key in sorted(plan.keys()):
                items.extend(plan[key])
            first_add = {}
            last_add = {}
            for k, item in enumerate(items):
                if item[0] == "add":
                    first_add.setdefault((item[1], item[2]), k)
                    last_add[(item[1], item[2])] = k
            with tc.manual_schedule():
                for k, item in enumerate(items):
                    if item[0] == "add":
                        grp = (item[1], item[2])
                        assert first_add[grp] != k or item[3] == 0
                        do_add(item[1], item[2], item[3], first_add[grp] == k, last_add[grp] == k)
                    else:
                        table[item[0]](*item[1:])
